import numpy as np
import ml_dtypes


def mxq(x, axis, fmt="e4m3"):
    dtype, down = {"e4m3": (ml_dtypes.float8_e4m3fn, 7), "e5m2": (ml_dtypes.float8_e5m2, 14)}[fmt]
    v = np.moveaxis(np.asarray(x, np.float32).astype(ml_dtypes.bfloat16).astype(np.float64), axis, -1)
    blocks = v.reshape(v.shape[:-1] + (-1, 32))
    amax = np.abs(blocks).max(-1, keepdims=True)
    byte = np.maximum(np.where(amax > 0, np.frexp(amax)[1] - 1 + 127, 0) - down, 1)
    scale = np.exp2(byte - 127.0)
    codes = (blocks / scale).astype(np.float32).astype(dtype).astype(np.float64)
    return np.moveaxis((codes * scale).reshape(v.shape), -1, axis)


WIDE = False


def mx_kscale(k):
    if not WIDE:
        return np.ones(k)
    levels = np.array([10, -10, 5, -5, 0])
    a = np.random.permutation(np.resize(levels, k // 512 * 4)).reshape(k // 512, 4)
    idx = np.arange(k)
    return np.exp2(a[idx // 512, idx % 128 // 32])


BF16 = ml_dtypes.bfloat16


def bf(x):
    return np.asarray(x, np.float32).astype(BF16)


def f64(x):
    return np.asarray(x).astype(np.float64)


E2M1 = np.array([0.0, 0.5, 1.0, 1.5, 2.0, 3.0, 4.0, 6.0, -0.0, -0.5, -1.0, -1.5, -2.0, -3.0, -4.0, -6.0])


def pack_weight(w, fmt):
    k, n = w.shape
    w = f64(bf(w)).reshape(k // 32, 32, n)
    amax = np.abs(w).max(1)
    if fmt == "e4m3":
        byte = np.frexp(amax)[1] - 1 + 127 - 7
    else:
        mant, ex = np.frexp(amax / 6.0)
        byte = np.where(mant > 0.5, ex, ex - 1) + 127
    byte = np.clip(np.where(amax > 0, byte, 1), 1, 254)
    scaled = (w * np.exp2(127.0 - byte)[:, None, :]).reshape(k, n).astype(np.float32)
    by_word = np.ascontiguousarray(scaled.reshape(k // 512, 128, 4, n).transpose(0, 1, 3, 2))
    if fmt == "e4m3":
        words = by_word.astype(ml_dtypes.float8_e4m3fn).view(np.uint8)
    else:
        c = by_word.astype(ml_dtypes.float4_e2m1fn).view(np.uint8) & 0xF
        words = c[..., 0::2] | (c[..., 1::2] << 4)
    return np.ascontiguousarray(words), np.ascontiguousarray(byte.astype(np.uint8).reshape(k // 512, 16, n))


def unpack_weight(words, scales, fmt):
    g, p, n, _ = words.shape
    if fmt == "e4m3":
        vals = np.ascontiguousarray(words).view(ml_dtypes.float8_e4m3fn).astype(np.float64)
    else:
        nib = np.empty((g, p, n, 4), np.uint8)
        nib[..., 0::2] = words & 0xF
        nib[..., 1::2] = words >> 4
        vals = E2M1[nib]
    vals = vals * np.repeat(np.exp2(scales.astype(np.float64) - 127.0), 8, axis=1)[..., None]
    return vals.transpose(0, 1, 3, 2).reshape(g * 512, n)

def pack4(w):
    words, scales = pack_weight(w, "e2m1")
    return words.reshape(words.shape[0], 128, -1), scales


def unpack4(words, scales):
    return unpack_weight(words.reshape(words.shape[0], 128, -1, 2), scales, "e2m1")


B, H, L, G, P = 128, 1024, 4, 4, 2


def sigmoid(v):
    return 1.0 / (1.0 + np.exp(-v))


def setup_inputs():
    s, t = mx_kscale(H), mx_kscale(H)
    sc = 1.0 / np.sqrt(H)
    lstm_input = bf(np.random.standard_normal((B, H)) * 0.5 * s)
    h_prev = bf(np.random.standard_normal((B, H)) * t)
    c_prev = bf(np.random.standard_normal((B, H)))
    w_ih = np.random.standard_normal((G * H, H)) * sc / s[None, :]
    w_hh = np.random.standard_normal((G * H, H)) * sc / t[None, :]
    b_ih = bf(np.random.standard_normal(G * H) * 0.3)
    b_hh = bf(np.random.standard_normal(G * H) * 0.3)
    w_ih_words, w_ih_scales = pack4(np.ascontiguousarray(w_ih.T))
    w_hh_words, w_hh_scales = pack4(np.ascontiguousarray(w_hh.T))
    return {"lstm_input": lstm_input,
            "h_prev": h_prev,
            "c_prev": c_prev,
            "w_ih_words": w_ih_words,
            "w_ih_scales": w_ih_scales,
            "w_hh_words": w_hh_words,
            "w_hh_scales": w_hh_scales,
            "b_ih": b_ih,
            "b_hh": b_hh}


def reference(lstm_input, h_prev, c_prev, w_ih_words, w_ih_scales, w_hh_words, w_hh_scales, b_ih, b_hh):
    gates = ((mxq(f64(lstm_input), 1, "e4m3") @ unpack4(w_ih_words, w_ih_scales)) + f64(b_ih)
             + (mxq(f64(h_prev), 1, "e4m3") @ unpack4(w_hh_words, w_hh_scales)) + f64(b_hh))
    i, f, g, o = np.split(gates, G, axis=-1)
    i = sigmoid(i)
    f = sigmoid(f)
    g = np.tanh(g)
    o = sigmoid(o)
    c_next = f * f64(c_prev) + i * g
    h_next = o * np.tanh(c_next)
    return h_next, c_next

@@ -1,0 +1,180 @@
+from contextlib import ExitStack
+
+import concourse.mybir as mybir
+from concourse.masks import make_identity
+
+F32 = mybir.dt.float32
+BF16 = mybir.dt.bfloat16
+I32 = mybir.dt.int32
+U32 = mybir.dt.uint32
+U8 = mybir.dt.uint8
+FP8X4 = mybir.dt.float8_e4m3fn_x4
+FP4X4 = mybir.dt.float4_e2m1fn_x4
+ACT = mybir.ActivationFunctionType
+
+P = 128
+H = 1024
+GATES = 4
+I_GATE, F_GATE, G_GATE, O_GATE = 0, 1, 2, 3
+INPUTS = 2
+K_PASS = 512
+GROUPS = H // K_PASS
+PASSES = INPUTS * GROUPS
+BANK = 512
+HALVES = H // BANK
+PSUM_BANKS = 8
+
+FLOPS = 2 * P * (INPUTS * H) * (GATES * H)
+
+
+def half(b):
+    return slice(b * BANK, (b + 1) * BANK)
+
+
+def tile_multilayerlstmcell_pa_kernel(
+    tc,
+    lstm_input,
+    h_prev,
+    c_prev,
+    w_ih_words,
+    w_ih_scales,
+    w_hh_words,
+    w_hh_scales,
+    b_ih,
+    b_hh,
+    out_0,
+    out_1,
+):
+    nc = tc.nc
+    words_in = (w_ih_words, w_hh_words)
+    scales_in = (w_ih_scales, w_hh_scales)
+
+    with ExitStack() as ctx:
+        keep = ctx.enter_context(tc.tile_pool(name="keep", bufs=1))
+        psum = ctx.enter_context(tc.psum_pool(name="psum", bufs=PSUM_BANKS))
+        ctx.enter_context(tc.manual_schedule())
+
+        acts = keep.tile([P, INPUTS, H], BF16)
+        nc.sync.dma_start(out=acts[:, 0, :], in_=lstm_input)
+        nc.sync.dma_start(out=acts[:, 1, :], in_=h_prev)
+
+        warm = keep.tile([P, 1], F32)
+        nc.vector.memset(warm[:], 0.0)
+        nc.scalar.activation(out=warm[:], in_=warm[:], func=ACT.Sigmoid)
+
+        w_planes = keep.tile([P, PASSES, GATES * H], U8, align_bytes=64)
+        for s in range(INPUTS):
+            nc.vector.memset(w_planes[:, GROUPS * s : GROUPS * (s + 1), :].bitcast(I32), 0)
+        for s in range(INPUTS):
+            for j in range(8):
+                first = 32 * (j // 4) + j % 4
+                nc.sync.dma_start(
+                    out=w_planes[first:P:64, GROUPS * s : GROUPS * (s + 1), :].bitcast(I32),
+                    in_=scales_in[s][:, j:16:8, :].rearrange("g j n -> j g n").bitcast(I32),
+                )
+
+        w_words = keep.tile([P, GATES, PASSES, 2 * H], U8, align_bytes=64)
+
+        def load_gate_words(q):
+            for c in range(PASSES):
+                nc.sync.dma_start(
+                    out=w_words[:, q, c, :].bitcast(I32),
+                    in_=words_in[c // GROUPS][c % GROUPS, :, 2 * H * q : 2 * H * (q + 1)].bitcast(I32),
+                )
+
+        c_old = keep.tile([P, H], BF16)
+        load_gate_words(F_GATE)
+        nc.sync.dma_start(out=c_old[:], in_=c_prev)
+        load_gate_words(I_GATE)
+        load_gate_words(G_GATE)
+        load_gate_words(O_GATE)
+
+        bias_rows = keep.tile([P, GATES * H], BF16)
+        nc.vector.memset(bias_rows[:].bitcast(I32), 0)
+        nc.scalar.dma_start(out=bias_rows[0:1, :], in_=b_ih.rearrange("(o n) -> o n", o=1))
+        nc.scalar.dma_start(out=bias_rows[1:2, :], in_=b_hh.rearrange("(o n) -> o n", o=1))
+        ones = keep.tile([P, P], BF16)
+        nc.vector.memset(ones[:], 1.0)
+        ident = keep.tile([P, P], F32)
+        make_identity(nc, ident[:])
+
+        grouped = keep.tile([P, INPUTS, GROUPS, P, 4], BF16, align_bytes=64)
+        x_codes = keep.tile([P, PASSES, P], U32, align_bytes=64)
+        x_planes = keep.tile([P, PASSES, P], U8, align_bytes=64)
+        for s in range(INPUTS):
+            in_words = acts[:, s, :].bitcast(F32)
+            turned = psum.tile([P, BANK], F32, name="turned", tag="bank")
+            turned_gum = turned[:].rearrange("p (g u m) -> p g u m", g=GROUPS, u=2)
+            for g in range(GROUPS):
+                for u in range(2):
+                    nc.tensor.transpose(
+                        turned_gum[:, g, u, :],
+                        in_words[:, 256 * g + u : 256 * (g + 1) : 2],
+                        ident[:],
+                    )
+            nc.vector.tensor_copy(
+                out=grouped[:, s].bitcast(F32),
+                in_=turned_gum.rearrange("p g u m -> p g m u"),
+            )
+        for s in range(INPUTS):
+            passes = slice(GROUPS * s, GROUPS * (s + 1))
+            nc.vector.quantize_mx(
+                out=x_codes[:, passes, :].rearrange("p c m -> p (c m)").bitcast(FP8X4),
+                scales=x_planes[:, passes, :].rearrange("p c m -> p (c m)"),
+                in_=grouped[:, s].rearrange("p g m t -> p (g m t)"),
+            )
+
+        gates = keep.tile([P, GATES, H], F32)
+        for q in (F_GATE, I_GATE, G_GATE, O_GATE):
+            for b in range(HALVES):
+                spread = psum.tile([P, BANK], F32, name="spread", tag="bank")
+                nc.tensor.matmul(
+                    out=spread[:],
+                    lhsT=ones[:],
+                    rhs=bias_rows[:, H * q + BANK * b : H * q + BANK * (b + 1)],
+                    start=True,
+                    stop=True,
+                )
+                nc.scalar.copy(out=gates[:, q, half(b)], in_=spread[:])
+
+        def gate(q, func):
+            sums = [psum.tile([P, BANK], F32, name="sums%d" % b, tag="bank") for b in range(HALVES)]
+            for c in range(PASSES):
+                for b in range(HALVES):
+                    nc.tensor.matmul_mx(
+                        out=sums[b][:],
+                        lhsT=x_codes[:, c, :].bitcast(FP8X4),
+                        lhsT_scale=x_planes[:, c, :],
+                        rhs=w_words[:, q, c, 2 * BANK * b : 2 * BANK * (b + 1)].bitcast(FP4X4),
+                        rhs_scale=w_planes[:, c, H * q + BANK * b : H * q + BANK * (b + 1)],
+                        start=(c == 0),
+                        stop=(c == PASSES - 1),
+                    )
+            for b in range(HALVES):
+                nc.vector.tensor_add(out=gates[:, q, half(b)], in0=sums[b][:], in1=gates[:, q, half(b)])
+            for b in range(HALVES):
+                nc.scalar.activation(out=gates[:, q, half(b)], in_=gates[:, q, half(b)], func=func)
+            return gates[:, q, :]
+
+        cell = keep.tile([P, H], F32)
+        cell_tanh = keep.tile([P, H], F32)
+        hidden = keep.tile([P, H], F32)
+
+        forget = gate(F_GATE, ACT.Sigmoid)
+        for b in range(HALVES):
+            nc.vector.tensor_mul(out=cell[:, half(b)], in0=forget[:, half(b)], in1=c_old[:, half(b)])
+
+        admit = gate(I_GATE, ACT.Sigmoid)
+
+        fresh = gate(G_GATE, ACT.Tanh)
+        for b in range(HALVES):
+            nc.vector.tensor_mul(out=fresh[:, half(b)], in0=admit[:, half(b)], in1=fresh[:, half(b)])
+        for b in range(HALVES):
+            nc.vector.tensor_add(out=cell[:, half(b)], in0=cell[:, half(b)], in1=fresh[:, half(b)])
+            nc.scalar.activation(out=cell_tanh[:, half(b)], in_=cell[:, half(b)], func=ACT.Tanh)
+            nc.sync.dma_start(out=out_1[:, half(b)], in_=cell[:, half(b)])
+
+        expose = gate(O_GATE, ACT.Sigmoid)
+        for b in range(HALVES):
+            nc.vector.tensor_mul(out=hidden[:, half(b)], in0=expose[:, half(b)], in1=cell_tanh[:, half(b)])
+            nc.sync.dma_start(out=out_0[:, half(b)], in_=hidden[:, half(b)])

@@ -65,6 +65,16 @@ def tile_multilayerlstmcell_pa_kernel(
         w_planes = keep.tile([P, PASSES, GATES * H], U8, align_bytes=64)
         for s in range(INPUTS):
             nc.vector.memset(w_planes[:, GROUPS * s : GROUPS * (s + 1), :].bitcast(I32), 0)
+
+        ident = keep.tile([P, P], F32)
+        make_identity(nc, ident[:])
+        bias_rows = keep.tile([P, GATES * H], BF16)
+        nc.vector.memset(bias_rows[:].bitcast(I32), 0)
+        nc.gpsimd.dma_start(out=bias_rows[0:1, :], in_=b_ih.rearrange("(o n) -> o n", o=1))
+        nc.gpsimd.dma_start(out=bias_rows[1:2, :], in_=b_hh.rearrange("(o n) -> o n", o=1))
+        ones = keep.tile([P, P], BF16)
+        nc.vector.memset(ones[:], 1.0)
+
         for s in range(INPUTS):
             for j in range(8):
                 first = 32 * (j // 4) + j % 4
@@ -88,15 +98,6 @@ def tile_multilayerlstmcell_pa_kernel(
         load_gate_words(I_GATE)
         load_gate_words(G_GATE)
         load_gate_words(O_GATE)
-
-        bias_rows = keep.tile([P, GATES * H], BF16)
-        nc.vector.memset(bias_rows[:].bitcast(I32), 0)
-        nc.scalar.dma_start(out=bias_rows[0:1, :], in_=b_ih.rearrange("(o n) -> o n", o=1))
-        nc.scalar.dma_start(out=bias_rows[1:2, :], in_=b_hh.rearrange("(o n) -> o n", o=1))
-        ones = keep.tile([P, P], BF16)
-        nc.vector.memset(ones[:], 1.0)
-        ident = keep.tile([P, P], F32)
-        make_identity(nc, ident[:])
 
         grouped = keep.tile([P, INPUTS, GROUPS, P, 4], BF16, align_bytes=64)
         x_codes = keep.tile([P, PASSES, P], U32, align_bytes=64)

@@ -23,6 +23,7 @@ PASSES = INPUTS * GROUPS
 BANK = 512
 HALVES = H // BANK
 PSUM_BANKS = 8
+QUADRANT = 32
 
 FLOPS = 2 * P * (INPUTS * H) * (GATES * H)
 
@@ -58,6 +59,11 @@ def tile_multilayerlstmcell_pa_kernel(
         nc.sync.dma_start(out=acts[:, 0, :], in_=lstm_input)
         nc.sync.dma_start(out=acts[:, 1, :], in_=h_prev)
 
+        bias_rows = keep.tile([P, H], BF16)
+        nc.vector.memset(bias_rows[:].bitcast(I32), 0)
+        nc.sync.dma_start(out=bias_rows[0:P:QUADRANT, :], in_=b_ih.rearrange("(q n) -> q n", q=GATES))
+        nc.sync.dma_start(out=bias_rows[1:P:QUADRANT, :], in_=b_hh.rearrange("(q n) -> q n", q=GATES))
+
         warm = keep.tile([P, 1], F32)
         nc.vector.memset(warm[:], 0.0)
         nc.scalar.activation(out=warm[:], in_=warm[:], func=ACT.Sigmoid)
@@ -66,38 +72,44 @@ def tile_multilayerlstmcell_pa_kernel(
         for s in range(INPUTS):
             nc.vector.memset(w_planes[:, GROUPS * s : GROUPS * (s + 1), :].bitcast(I32), 0)
 
+        pick = keep.tile([P, GATES, P], BF16)
+        nc.vector.memset(pick[:].bitcast(I32), 0)
+        for q in range(GATES):
+            nc.vector.memset(pick[QUADRANT * q : QUADRANT * (q + 1), q, :], 1.0)
         ident = keep.tile([P, P], F32)
         make_identity(nc, ident[:])
-        bias_rows = keep.tile([P, GATES * H], BF16)
-        nc.vector.memset(bias_rows[:].bitcast(I32), 0)
-        nc.gpsimd.dma_start(out=bias_rows[0:1, :], in_=b_ih.rearrange("(o n) -> o n", o=1))
-        nc.gpsimd.dma_start(out=bias_rows[1:2, :], in_=b_hh.rearrange("(o n) -> o n", o=1))
-        ones = keep.tile([P, P], BF16)
-        nc.vector.memset(ones[:], 1.0)
 
-        for s in range(INPUTS):
-            for j in range(8):
+        def load_scale_rows(s, cols, apart):
+            for j in range(apart // 8):
                 first = 32 * (j // 4) + j % 4
                 nc.sync.dma_start(
-                    out=w_planes[first:P:64, GROUPS * s : GROUPS * (s + 1), :].bitcast(I32),
-                    in_=scales_in[s][:, j:16:8, :].rearrange("g j n -> j g n").bitcast(I32),
+                    out=w_planes[first:P:apart, GROUPS * s : GROUPS * (s + 1), cols].bitcast(I32),
+                    in_=scales_in[s][:, j : 16 : apart // 8, cols].rearrange("g j n -> j g n").bitcast(I32),
                 )
+
+        for s in range(INPUTS):
+            load_scale_rows(s, slice(0, O_GATE * H), 64)
 
         w_words = keep.tile([P, GATES, PASSES, 2 * H], U8, align_bytes=64)
 
-        def load_gate_words(q):
-            for c in range(PASSES):
+        def load_gate_words(q, s):
+            for g in range(GROUPS):
                 nc.sync.dma_start(
-                    out=w_words[:, q, c, :].bitcast(I32),
-                    in_=words_in[c // GROUPS][c % GROUPS, :, 2 * H * q : 2 * H * (q + 1)].bitcast(I32),
+                    out=w_words[:, q, GROUPS * s + g, :].bitcast(I32),
+                    in_=words_in[s][g, :, 2 * H * q : 2 * H * (q + 1)].bitcast(I32),
                 )
 
         c_old = keep.tile([P, H], BF16)
-        load_gate_words(F_GATE)
+        for s in range(INPUTS):
+            load_gate_words(F_GATE, s)
         nc.sync.dma_start(out=c_old[:], in_=c_prev)
-        load_gate_words(I_GATE)
-        load_gate_words(G_GATE)
-        load_gate_words(O_GATE)
+        for s in range(INPUTS):
+            load_gate_words(I_GATE, s)
+        for s in range(INPUTS):
+            load_gate_words(G_GATE, s)
+        for s in range(INPUTS):
+            load_scale_rows(s, slice(O_GATE * H, GATES * H), 32)
+            load_gate_words(O_GATE, s)
 
         grouped = keep.tile([P, INPUTS, GROUPS, P, 4], BF16, align_bytes=64)
         x_codes = keep.tile([P, PASSES, P], U32, align_bytes=64)
@@ -131,8 +143,8 @@ def tile_multilayerlstmcell_pa_kernel(
                 spread = psum.tile([P, BANK], F32, name="spread", tag="bank")
                 nc.tensor.matmul(
                     out=spread[:],
-                    lhsT=ones[:],
-                    rhs=bias_rows[:, H * q + BANK * b : H * q + BANK * (b + 1)],
+                    lhsT=pick[:, q, :],
+                    rhs=bias_rows[:, half(b)],
                     start=True,
                     stop=True,
                 )

@@ -68,9 +68,11 @@ def tile_multilayerlstmcell_pa_kernel(
         nc.vector.memset(warm[:], 0.0)
         nc.scalar.activation(out=warm[:], in_=warm[:], func=ACT.Sigmoid)
 
-        w_planes = keep.tile([P, PASSES, GATES * H], U8, align_bytes=64)
+        early_planes = keep.tile([P, PASSES, O_GATE * H], U8, align_bytes=64)
+        late_planes = keep.tile([P, PASSES, H], U8, align_bytes=64)
         for s in range(INPUTS):
-            nc.vector.memset(w_planes[:, GROUPS * s : GROUPS * (s + 1), :].bitcast(I32), 0)
+            nc.vector.memset(early_planes[:, GROUPS * s : GROUPS * (s + 1), :].bitcast(I32), 0)
+        nc.vector.memset(late_planes[:].bitcast(I32), 0)
 
         pick = keep.tile([P, GATES, P], BF16)
         nc.vector.memset(pick[:].bitcast(I32), 0)
@@ -79,16 +81,16 @@ def tile_multilayerlstmcell_pa_kernel(
         ident = keep.tile([P, P], F32)
         make_identity(nc, ident[:])
 
-        def load_scale_rows(s, cols, apart):
+        def load_scale_rows(planes, s, cols, apart):
             for j in range(apart // 8):
                 first = 32 * (j // 4) + j % 4
                 nc.sync.dma_start(
-                    out=w_planes[first:P:apart, GROUPS * s : GROUPS * (s + 1), cols].bitcast(I32),
+                    out=planes[first:P:apart, GROUPS * s : GROUPS * (s + 1), :].bitcast(I32),
                     in_=scales_in[s][:, j : 16 : apart // 8, cols].rearrange("g j n -> j g n").bitcast(I32),
                 )
 
         for s in range(INPUTS):
-            load_scale_rows(s, slice(0, O_GATE * H), 64)
+            load_scale_rows(early_planes, s, slice(0, O_GATE * H), 64)
 
         w_words = keep.tile([P, GATES, PASSES, 2 * H], U8, align_bytes=64)
 
@@ -108,7 +110,7 @@ def tile_multilayerlstmcell_pa_kernel(
         for s in range(INPUTS):
             load_gate_words(G_GATE, s)
         for s in range(INPUTS):
-            load_scale_rows(s, slice(O_GATE * H, GATES * H), 32)
+            load_scale_rows(late_planes, s, slice(O_GATE * H, GATES * H), 32)
             load_gate_words(O_GATE, s)
 
         grouped = keep.tile([P, INPUTS, GROUPS, P, 4], BF16, align_bytes=64)
@@ -151,6 +153,7 @@ def tile_multilayerlstmcell_pa_kernel(
                 nc.scalar.copy(out=gates[:, q, half(b)], in_=spread[:])
 
         def gate(q, func):
+            planes, first_col = (late_planes, 0) if q == O_GATE else (early_planes, H * q)
             sums = [psum.tile([P, BANK], F32, name="sums%d" % b, tag="bank") for b in range(HALVES)]
             for c in range(PASSES):
                 for b in range(HALVES):
@@ -159,7 +162,7 @@ def tile_multilayerlstmcell_pa_kernel(
                         lhsT=x_codes[:, c, :].bitcast(FP8X4),
                         lhsT_scale=x_planes[:, c, :],
                         rhs=w_words[:, q, c, 2 * BANK * b : 2 * BANK * (b + 1)].bitcast(FP4X4),
-                        rhs_scale=w_planes[:, c, H * q + BANK * b : H * q + BANK * (b + 1)],
+                        rhs_scale=planes[:, c, first_col + BANK * b : first_col + BANK * (b + 1)],
                         start=(c == 0),
                         stop=(c == PASSES - 1),
                     )

@@ -90,7 +90,7 @@ def tile_multilayerlstmcell_pa_kernel(
                 )
 
         for s in range(INPUTS):
-            load_scale_rows(early_planes, s, slice(0, O_GATE * H), 64)
+            load_scale_rows(early_planes, s, slice(0, O_GATE * H), 32)
 
         w_words = keep.tile([P, GATES, PASSES, 2 * H], U8, align_bytes=64)
 

@@ -92,26 +92,29 @@ def tile_multilayerlstmcell_pa_kernel(
         for s in range(INPUTS):
             load_scale_rows(early_planes, s, slice(0, O_GATE * H), 32)
 
-        w_words = keep.tile([P, GATES, PASSES, 2 * H], U8, align_bytes=64)
+        w_words = keep.tile([P, GATES, HALVES, PASSES, 2 * BANK], U8, align_bytes=64)
 
-        def load_gate_words(q, s):
-            for g in range(GROUPS):
-                nc.sync.dma_start(
-                    out=w_words[:, q, GROUPS * s + g, :].bitcast(I32),
-                    in_=words_in[s][g, :, 2 * H * q : 2 * H * (q + 1)].bitcast(I32),
-                )
+        def load_half_words(q, b, s):
+            first = 2 * H * q + 2 * BANK * b
+            nc.sync.dma_start(
+                out=w_words[:, q, b, GROUPS * s : GROUPS * (s + 1), :].bitcast(I32),
+                in_=words_in[s][:, :, first : first + 2 * BANK].rearrange("g p n -> p g n").bitcast(I32),
+            )
 
         c_old = keep.tile([P, H], BF16)
-        for s in range(INPUTS):
-            load_gate_words(F_GATE, s)
+        for b in range(HALVES):
+            for s in range(INPUTS):
+                load_half_words(F_GATE, b, s)
         nc.sync.dma_start(out=c_old[:], in_=c_prev)
-        for s in range(INPUTS):
-            load_gate_words(I_GATE, s)
-        for s in range(INPUTS):
-            load_gate_words(G_GATE, s)
+        for q in (I_GATE, G_GATE):
+            for b in range(HALVES):
+                for s in range(INPUTS):
+                    load_half_words(q, b, s)
         for s in range(INPUTS):
             load_scale_rows(late_planes, s, slice(O_GATE * H, GATES * H), 32)
-            load_gate_words(O_GATE, s)
+            load_half_words(O_GATE, 0, s)
+        for s in range(INPUTS):
+            load_half_words(O_GATE, 1, s)
 
         grouped = keep.tile([P, INPUTS, GROUPS, P, 4], BF16, align_bytes=64)
         x_codes = keep.tile([P, PASSES, P], U32, align_bytes=64)
@@ -152,45 +155,47 @@ def tile_multilayerlstmcell_pa_kernel(
                 )
                 nc.scalar.copy(out=gates[:, q, half(b)], in_=spread[:])
 
-        def gate(q, func):
+        def sums_of(q, b):
             planes, first_col = (late_planes, 0) if q == O_GATE else (early_planes, H * q)
-            sums = [psum.tile([P, BANK], F32, name="sums%d" % b, tag="bank") for b in range(HALVES)]
+            sums = psum.tile([P, BANK], F32, name="sums", tag="bank")
             for c in range(PASSES):
-                for b in range(HALVES):
-                    nc.tensor.matmul_mx(
-                        out=sums[b][:],
-                        lhsT=x_codes[:, c, :].bitcast(FP8X4),
-                        lhsT_scale=x_planes[:, c, :],
-                        rhs=w_words[:, q, c, 2 * BANK * b : 2 * BANK * (b + 1)].bitcast(FP4X4),
-                        rhs_scale=planes[:, c, first_col + BANK * b : first_col + BANK * (b + 1)],
-                        start=(c == 0),
-                        stop=(c == PASSES - 1),
-                    )
-            for b in range(HALVES):
-                nc.vector.tensor_add(out=gates[:, q, half(b)], in0=sums[b][:], in1=gates[:, q, half(b)])
-            for b in range(HALVES):
-                nc.scalar.activation(out=gates[:, q, half(b)], in_=gates[:, q, half(b)], func=func)
-            return gates[:, q, :]
+                nc.tensor.matmul_mx(
+                    out=sums[:],
+                    lhsT=x_codes[:, c, :].bitcast(FP8X4),
+                    lhsT_scale=x_planes[:, c, :],
+                    rhs=w_words[:, q, b, c, :].bitcast(FP4X4),
+                    rhs_scale=planes[:, c, first_col + BANK * b : first_col + BANK * (b + 1)],
+                    start=(c == 0),
+                    stop=(c == PASSES - 1),
+                )
+            return sums
+
+        def gate_half(q, b, func):
+            sums = sums_of(q, b)
+            nc.vector.tensor_add(out=gates[:, q, half(b)], in0=sums[:], in1=gates[:, q, half(b)])
+            nc.scalar.activation(out=gates[:, q, half(b)], in_=gates[:, q, half(b)], func=func)
 
         cell = keep.tile([P, H], F32)
         cell_tanh = keep.tile([P, H], F32)
         hidden = keep.tile([P, H], F32)
+        forget, admit, fresh, expose = [gates[:, q, :] for q in (F_GATE, I_GATE, G_GATE, O_GATE)]
 
-        forget = gate(F_GATE, ACT.Sigmoid)
+        for b in range(HALVES):
+            gate_half(F_GATE, b, ACT.Sigmoid)
         for b in range(HALVES):
             nc.vector.tensor_mul(out=cell[:, half(b)], in0=forget[:, half(b)], in1=c_old[:, half(b)])
-
-        admit = gate(I_GATE, ACT.Sigmoid)
-
-        fresh = gate(G_GATE, ACT.Tanh)
+        for b in range(HALVES):
+            gate_half(I_GATE, b, ACT.Sigmoid)
+        for b in range(HALVES):
+            gate_half(G_GATE, b, ACT.Tanh)
         for b in range(HALVES):
             nc.vector.tensor_mul(out=fresh[:, half(b)], in0=admit[:, half(b)], in1=fresh[:, half(b)])
         for b in range(HALVES):
             nc.vector.tensor_add(out=cell[:, half(b)], in0=cell[:, half(b)], in1=fresh[:, half(b)])
             nc.scalar.activation(out=cell_tanh[:, half(b)], in_=cell[:, half(b)], func=ACT.Tanh)
             nc.sync.dma_start(out=out_1[:, half(b)], in_=cell[:, half(b)])
-
-        expose = gate(O_GATE, ACT.Sigmoid)
+        for b in range(HALVES):
+            gate_half(O_GATE, b, ACT.Sigmoid)
         for b in range(HALVES):
             nc.vector.tensor_mul(out=hidden[:, half(b)], in0=expose[:, half(b)], in1=cell_tanh[:, half(b)])
             nc.sync.dma_start(out=out_0[:, half(b)], in_=hidden[:, half(b)])

@@ -21,6 +21,8 @@ K_PASS = 512
 GROUPS = H // K_PASS
 PASSES = INPUTS * GROUPS
 BANK = 512
+QUARTER = 256
+RUN = 128
 HALVES = H // BANK
 PSUM_BANKS = 8
 QUADRANT = 32
@@ -194,8 +196,41 @@ def tile_multilayerlstmcell_pa_kernel(
             nc.vector.tensor_add(out=cell[:, half(b)], in0=cell[:, half(b)], in1=fresh[:, half(b)])
             nc.scalar.activation(out=cell_tanh[:, half(b)], in_=cell[:, half(b)], func=ACT.Tanh)
             nc.sync.dma_start(out=out_1[:, half(b)], in_=cell[:, half(b)])
-        for b in range(HALVES):
-            gate_half(O_GATE, b, ACT.Sigmoid)
-        for b in range(HALVES):
-            nc.vector.tensor_mul(out=hidden[:, half(b)], in0=expose[:, half(b)], in1=cell_tanh[:, half(b)])
-            nc.sync.dma_start(out=out_0[:, half(b)], in_=hidden[:, half(b)])
+        gate_half(O_GATE, 0, ACT.Sigmoid)
+
+        runs = []
+        for r in range(BANK // RUN):
+            sums = psum.tile([P, RUN], F32, name="sums", tag="bank")
+            runs.append(sums)
+
+        def last_pass(r, c):
+            first = BANK + RUN * r
+            nc.tensor.matmul_mx(
+                out=runs[r][:],
+                lhsT=x_codes[:, c, :].bitcast(FP8X4),
+                lhsT_scale=x_planes[:, c, :],
+                rhs=w_words[:, O_GATE, 1, c, 2 * RUN * r : 2 * RUN * (r + 1)].bitcast(FP4X4),
+                rhs_scale=late_planes[:, c, first : first + RUN],
+                start=(c == 0),
+                stop=(c == PASSES - 1),
+            )
+
+        for r in range(BANK // RUN):
+            for c in range(GROUPS):
+                last_pass(r, c)
+        for r in range(BANK // RUN):
+            for c in range(GROUPS, PASSES):
+                last_pass(r, c)
+        pieces = [slice(BANK + QUARTER * k, BANK + QUARTER * (k + 1)) for k in range(BANK // QUARTER)]
+        for k, cols in enumerate(pieces):
+            for j in range(QUARTER // RUN):
+                first = cols.start + RUN * j
+                nc.vector.tensor_add(
+                    out=expose[:, first : first + RUN],
+                    in0=runs[k * (QUARTER // RUN) + j][:],
+                    in1=expose[:, first : first + RUN],
+                )
+            nc.scalar.activation(out=expose[:, cols], in_=expose[:, cols], func=ACT.Sigmoid)
+        for cols in [half(0)] + pieces:
+            nc.vector.tensor_mul(out=hidden[:, cols], in0=expose[:, cols], in1=cell_tanh[:, cols])
+            nc.sync.dma_start(out=out_0[:, cols], in_=hidden[:, cols])

@@ -108,8 +108,8 @@ def tile_multilayerlstmcell_pa_kernel(
             for s in range(INPUTS):
                 load_half_words(F_GATE, b, s)
         nc.sync.dma_start(out=c_old[:], in_=c_prev)
-        for q in (I_GATE, G_GATE):
-            for b in range(HALVES):
+        for b in range(HALVES):
+            for q in (I_GATE, G_GATE):
                 for s in range(INPUTS):
                     load_half_words(q, b, s)
         for s in range(INPUTS):
@@ -182,21 +182,30 @@ def tile_multilayerlstmcell_pa_kernel(
         hidden = keep.tile([P, H], F32)
         forget, admit, fresh, expose = [gates[:, q, :] for q in (F_GATE, I_GATE, G_GATE, O_GATE)]
 
-        for b in range(HALVES):
-            gate_half(F_GATE, b, ACT.Sigmoid)
-        for b in range(HALVES):
+        def keep_part(b):
             nc.vector.tensor_mul(out=cell[:, half(b)], in0=forget[:, half(b)], in1=c_old[:, half(b)])
-        for b in range(HALVES):
-            gate_half(I_GATE, b, ACT.Sigmoid)
-        for b in range(HALVES):
-            gate_half(G_GATE, b, ACT.Tanh)
-        for b in range(HALVES):
+
+        def new_part(b):
             nc.vector.tensor_mul(out=fresh[:, half(b)], in0=admit[:, half(b)], in1=fresh[:, half(b)])
-        for b in range(HALVES):
+
+        def next_cell(b):
             nc.vector.tensor_add(out=cell[:, half(b)], in0=cell[:, half(b)], in1=fresh[:, half(b)])
             nc.scalar.activation(out=cell_tanh[:, half(b)], in_=cell[:, half(b)], func=ACT.Tanh)
             nc.sync.dma_start(out=out_1[:, half(b)], in_=cell[:, half(b)])
+
+        gate_half(F_GATE, 0, ACT.Sigmoid)
+        gate_half(F_GATE, 1, ACT.Sigmoid)
+        gate_half(I_GATE, 0, ACT.Sigmoid)
+        keep_part(0)
+        gate_half(G_GATE, 0, ACT.Tanh)
+        keep_part(1)
+        gate_half(I_GATE, 1, ACT.Sigmoid)
+        new_part(0)
+        gate_half(G_GATE, 1, ACT.Tanh)
+        next_cell(0)
+        new_part(1)
         gate_half(O_GATE, 0, ACT.Sigmoid)
+        next_cell(1)
 
         runs = []
         for r in range(BANK // RUN):

@@ -26,6 +26,7 @@ RUN = 128
 HALVES = H // BANK
 PSUM_BANKS = 8
 QUADRANT = 32
+ROWS = 4
 
 FLOPS = 2 * P * (INPUTS * H) * (GATES * H)
 
@@ -74,25 +75,24 @@ def tile_multilayerlstmcell_pa_kernel(
         late_planes = keep.tile([P, PASSES, H], U8, align_bytes=64)
         for s in range(INPUTS):
             nc.vector.memset(early_planes[:, GROUPS * s : GROUPS * (s + 1), :].bitcast(I32), 0)
-        nc.vector.memset(late_planes[:].bitcast(I32), 0)
 
         pick = keep.tile([P, GATES, P], BF16)
-        nc.vector.memset(pick[:].bitcast(I32), 0)
-        for q in range(GATES):
-            nc.vector.memset(pick[QUADRANT * q : QUADRANT * (q + 1), q, :], 1.0)
         ident = keep.tile([P, P], F32)
         make_identity(nc, ident[:])
+        nc.gpsimd.memset(pick[:].bitcast(I32), 0)
+        for q in range(GATES):
+            nc.gpsimd.memset(pick[QUADRANT * q : QUADRANT * (q + 1), q, :], 1.0)
+        nc.gpsimd.memset(late_planes[:].bitcast(I32), 0)
 
-        def load_scale_rows(planes, s, cols, apart):
-            for j in range(apart // 8):
-                first = 32 * (j // 4) + j % 4
-                nc.sync.dma_start(
-                    out=planes[first:P:apart, GROUPS * s : GROUPS * (s + 1), :].bitcast(I32),
-                    in_=scales_in[s][:, j : 16 : apart // 8, cols].rearrange("g j n -> j g n").bitcast(I32),
-                )
+        def load_scale_rows(planes, s, j, cols):
+            nc.sync.dma_start(
+                out=planes[j:P:QUADRANT, GROUPS * s : GROUPS * (s + 1), :].bitcast(I32),
+                in_=scales_in[s][:, j : 16 : ROWS, cols].rearrange("g j n -> j g n").bitcast(I32),
+            )
 
         for s in range(INPUTS):
-            load_scale_rows(early_planes, s, slice(0, O_GATE * H), 32)
+            for j in range(ROWS):
+                load_scale_rows(early_planes, s, j, slice(0, O_GATE * H))
 
         w_words = keep.tile([P, GATES, HALVES, PASSES, 2 * BANK], U8, align_bytes=64)
 
@@ -108,15 +108,24 @@ def tile_multilayerlstmcell_pa_kernel(
             for s in range(INPUTS):
                 load_half_words(F_GATE, b, s)
         nc.sync.dma_start(out=c_old[:], in_=c_prev)
-        for b in range(HALVES):
-            for q in (I_GATE, G_GATE):
-                for s in range(INPUTS):
-                    load_half_words(q, b, s)
-        for s in range(INPUTS):
-            load_scale_rows(late_planes, s, slice(O_GATE * H, GATES * H), 32)
-            load_half_words(O_GATE, 0, s)
-        for s in range(INPUTS):
-            load_half_words(O_GATE, 1, s)
+        for q in (I_GATE, G_GATE):
+            for s in range(INPUTS):
+                load_half_words(q, 0, s)
+        o_rows = [(s, j) for s in range(INPUTS) for j in range(ROWS)]
+        for (q, b, s), count in [
+            ((I_GATE, 1, 0), 1),
+            ((I_GATE, 1, 1), 1),
+            ((G_GATE, 1, 0), 2),
+            ((G_GATE, 1, 1), 2),
+            ((O_GATE, 0, 0), 2),
+            ((O_GATE, 0, 1), 0),
+            ((O_GATE, 1, 0), 0),
+            ((O_GATE, 1, 1), 0),
+        ]:
+            load_half_words(q, b, s)
+            for row in o_rows[:count]:
+                load_scale_rows(late_planes, *row, slice(O_GATE * H, GATES * H))
+            o_rows = o_rows[count:]
 
         grouped = keep.tile([P, INPUTS, GROUPS, P, 4], BF16, align_bytes=64)
         x_codes = keep.tile([P, PASSES, P], U32, align_bytes=64)

@@ -27,6 +27,8 @@ HALVES = H // BANK
 PSUM_BANKS = 8
 QUADRANT = 32
 ROWS = 4
+ROW = 256
+BIAS_ROWS = GATES * H // ROW
 
 FLOPS = 2 * P * (INPUTS * H) * (GATES * H)
 
@@ -62,10 +64,13 @@ def tile_multilayerlstmcell_pa_kernel(
         nc.sync.dma_start(out=acts[:, 0, :], in_=lstm_input)
         nc.sync.dma_start(out=acts[:, 1, :], in_=h_prev)
 
-        bias_rows = keep.tile([P, H], BF16)
+        bias_rows = keep.tile([P, ROW], BF16)
         nc.vector.memset(bias_rows[:].bitcast(I32), 0)
-        nc.sync.dma_start(out=bias_rows[0:P:QUADRANT, :], in_=b_ih.rearrange("(q n) -> q n", q=GATES))
-        nc.sync.dma_start(out=bias_rows[1:P:QUADRANT, :], in_=b_hh.rearrange("(q n) -> q n", q=GATES))
+        for k, bias in enumerate((b_ih, b_hh)):
+            nc.sync.dma_start(
+                out=bias_rows[BIAS_ROWS * k : BIAS_ROWS * (k + 1), :],
+                in_=bias.rearrange("(r n) -> r n", r=BIAS_ROWS),
+            )
 
         warm = keep.tile([P, 1], F32)
         nc.vector.memset(warm[:], 0.0)
@@ -76,12 +81,10 @@ def tile_multilayerlstmcell_pa_kernel(
         for s in range(INPUTS):
             nc.vector.memset(early_planes[:, GROUPS * s : GROUPS * (s + 1), :].bitcast(I32), 0)
 
-        pick = keep.tile([P, GATES, P], BF16)
         ident = keep.tile([P, P], F32)
         make_identity(nc, ident[:])
-        nc.gpsimd.memset(pick[:].bitcast(I32), 0)
-        for q in range(GATES):
-            nc.gpsimd.memset(pick[QUADRANT * q : QUADRANT * (q + 1), q, :], 1.0)
+        pick = keep.tile([P, BIAS_ROWS], BF16)
+        nc.gpsimd.tensor_add(out=pick[:], in0=ident[:, 0:BIAS_ROWS], in1=ident[:, BIAS_ROWS : 2 * BIAS_ROWS])
         nc.gpsimd.memset(late_planes[:].bitcast(I32), 0)
 
         def load_scale_rows(planes, s, j, cols):
@@ -157,13 +160,15 @@ def tile_multilayerlstmcell_pa_kernel(
         for q in (F_GATE, I_GATE, G_GATE, O_GATE):
             for b in range(HALVES):
                 spread = psum.tile([P, BANK], F32, name="spread", tag="bank")
-                nc.tensor.matmul(
-                    out=spread[:],
-                    lhsT=pick[:, q, :],
-                    rhs=bias_rows[:, half(b)],
-                    start=True,
-                    stop=True,
-                )
+                for k in range(BANK // ROW):
+                    r = (H * q + BANK * b) // ROW + k
+                    nc.tensor.matmul(
+                        out=spread[:, ROW * k : ROW * (k + 1)],
+                        lhsT=pick[:, r : r + 1].to_broadcast([P, P]),
+                        rhs=bias_rows[:],
+                        start=True,
+                        stop=True,
+                    )
                 nc.scalar.copy(out=gates[:, q, half(b)], in_=spread[:])
 
         def sums_of(q, b):

from contextlib import ExitStack

import concourse.mybir as mybir
from concourse.masks import make_identity

F32 = mybir.dt.float32
BF16 = mybir.dt.bfloat16
I32 = mybir.dt.int32
U32 = mybir.dt.uint32
U8 = mybir.dt.uint8
FP8X4 = mybir.dt.float8_e4m3fn_x4
FP4X4 = mybir.dt.float4_e2m1fn_x4
ACT = mybir.ActivationFunctionType

P = 128
H = 1024
GATES = 4
I_GATE, F_GATE, G_GATE, O_GATE = 0, 1, 2, 3
INPUTS = 2
K_PASS = 512
GROUPS = H // K_PASS
PASSES = INPUTS * GROUPS
BANK = 512
QUARTER = 256
RUN = 128
HALVES = H // BANK
PSUM_BANKS = 8
QUADRANT = 32
ROWS = 4
ROW = 256
BIAS_ROWS = GATES * H // ROW

FLOPS = 2 * P * (INPUTS * H) * (GATES * H)


def half(b):
    return slice(b * BANK, (b + 1) * BANK)


def tile_multilayerlstmcell_pa_kernel(
    tc,
    lstm_input,
    h_prev,
    c_prev,
    w_ih_words,
    w_ih_scales,
    w_hh_words,
    w_hh_scales,
    b_ih,
    b_hh,
    out_0,
    out_1,
):
    nc = tc.nc
    words_in = (w_ih_words, w_hh_words)
    scales_in = (w_ih_scales, w_hh_scales)

    with ExitStack() as ctx:
        keep = ctx.enter_context(tc.tile_pool(name="keep", bufs=1))
        psum = ctx.enter_context(tc.psum_pool(name="psum", bufs=PSUM_BANKS))
        ctx.enter_context(tc.manual_schedule())

        acts = keep.tile([P, INPUTS, H], BF16)
        nc.sync.dma_start(out=acts[:, 0, :], in_=lstm_input)
        nc.sync.dma_start(out=acts[:, 1, :], in_=h_prev)

        bias_rows = keep.tile([P, ROW], BF16)
        nc.vector.memset(bias_rows[:].bitcast(I32), 0)
        for k, bias in enumerate((b_ih, b_hh)):
            nc.sync.dma_start(
                out=bias_rows[BIAS_ROWS * k : BIAS_ROWS * (k + 1), :],
                in_=bias.rearrange("(r n) -> r n", r=BIAS_ROWS),
            )

        warm = keep.tile([P, 1], F32)
        nc.vector.memset(warm[:], 0.0)
        nc.scalar.activation(out=warm[:], in_=warm[:], func=ACT.Sigmoid)

        early_planes = keep.tile([P, PASSES, O_GATE * H], U8, align_bytes=64)
        late_planes = keep.tile([P, PASSES, H], U8, align_bytes=64)
        for s in range(INPUTS):
            nc.vector.memset(early_planes[:, GROUPS * s : GROUPS * (s + 1), :].bitcast(I32), 0)

        ident = keep.tile([P, P], F32)
        make_identity(nc, ident[:])
        pick = keep.tile([P, BIAS_ROWS], BF16)
        nc.gpsimd.tensor_add(out=pick[:], in0=ident[:, 0:BIAS_ROWS], in1=ident[:, BIAS_ROWS : 2 * BIAS_ROWS])
        nc.gpsimd.memset(late_planes[:].bitcast(I32), 0)

        def load_scale_rows(planes, s, j, cols):
            nc.sync.dma_start(
                out=planes[j:P:QUADRANT, GROUPS * s : GROUPS * (s + 1), :].bitcast(I32),
                in_=scales_in[s][:, j : 16 : ROWS, cols].rearrange("g j n -> j g n").bitcast(I32),
            )

        for s in range(INPUTS):
            for j in range(ROWS):
                load_scale_rows(early_planes, s, j, slice(0, O_GATE * H))

        w_words = keep.tile([P, GATES, HALVES, PASSES, 2 * BANK], U8, align_bytes=64)

        def load_half_words(q, b, s):
            first = 2 * H * q + 2 * BANK * b
            nc.sync.dma_start(
                out=w_words[:, q, b, GROUPS * s : GROUPS * (s + 1), :].bitcast(I32),
                in_=words_in[s][:, :, first : first + 2 * BANK].rearrange("g p n -> p g n").bitcast(I32),
            )

        c_old = keep.tile([P, H], BF16)
        for b in range(HALVES):
            for s in range(INPUTS):
                load_half_words(F_GATE, b, s)
        nc.sync.dma_start(out=c_old[:], in_=c_prev)
        for q in (I_GATE, G_GATE):
            for s in range(INPUTS):
                load_half_words(q, 0, s)
        o_rows = [(s, j) for s in range(INPUTS) for j in range(ROWS)]
        for (q, b, s), count in [
            ((I_GATE, 1, 0), 1),
            ((I_GATE, 1, 1), 1),
            ((G_GATE, 1, 0), 2),
            ((G_GATE, 1, 1), 2),
            ((O_GATE, 0, 0), 2),
            ((O_GATE, 0, 1), 0),
            ((O_GATE, 1, 0), 0),
            ((O_GATE, 1, 1), 0),
        ]:
            load_half_words(q, b, s)
            for row in o_rows[:count]:
                load_scale_rows(late_planes, *row, slice(O_GATE * H, GATES * H))
            o_rows = o_rows[count:]

        grouped = keep.tile([P, INPUTS, GROUPS, P, 4], BF16, align_bytes=64)
        x_codes = keep.tile([P, PASSES, P], U32, align_bytes=64)
        x_planes = keep.tile([P, PASSES, P], U8, align_bytes=64)
        for s in range(INPUTS):
            in_words = acts[:, s, :].bitcast(F32)
            turned = psum.tile([P, BANK], F32, name="turned", tag="bank")
            turned_gum = turned[:].rearrange("p (g u m) -> p g u m", g=GROUPS, u=2)
            for g in range(GROUPS):
                for u in range(2):
                    nc.tensor.transpose(
                        turned_gum[:, g, u, :],
                        in_words[:, 256 * g + u : 256 * (g + 1) : 2],
                        ident[:],
                    )
            nc.vector.tensor_copy(
                out=grouped[:, s].bitcast(F32),
                in_=turned_gum.rearrange("p g u m -> p g m u"),
            )
        for s in range(INPUTS):
            passes = slice(GROUPS * s, GROUPS * (s + 1))
            nc.vector.quantize_mx(
                out=x_codes[:, passes, :].rearrange("p c m -> p (c m)").bitcast(FP8X4),
                scales=x_planes[:, passes, :].rearrange("p c m -> p (c m)"),
                in_=grouped[:, s].rearrange("p g m t -> p (g m t)"),
            )

        gates = keep.tile([P, GATES, H], F32)
        for q in (F_GATE, I_GATE, G_GATE, O_GATE):
            for b in range(HALVES):
                spread = psum.tile([P, BANK], F32, name="spread", tag="bank")
                for k in range(BANK // ROW):
                    r = (H * q + BANK * b) // ROW + k
                    nc.tensor.matmul(
                        out=spread[:, ROW * k : ROW * (k + 1)],
                        lhsT=pick[:, r : r + 1].to_broadcast([P, P]),
                        rhs=bias_rows[:],
                        start=True,
                        stop=True,
                    )
                nc.scalar.copy(out=gates[:, q, half(b)], in_=spread[:])

        def sums_of(q, b):
            planes, first_col = (late_planes, 0) if q == O_GATE else (early_planes, H * q)
            sums = psum.tile([P, BANK], F32, name="sums", tag="bank")
            for c in range(PASSES):
                nc.tensor.matmul_mx(
                    out=sums[:],
                    lhsT=x_codes[:, c, :].bitcast(FP8X4),
                    lhsT_scale=x_planes[:, c, :],
                    rhs=w_words[:, q, b, c, :].bitcast(FP4X4),
                    rhs_scale=planes[:, c, first_col + BANK * b : first_col + BANK * (b + 1)],
                    start=(c == 0),
                    stop=(c == PASSES - 1),
                )
            return sums

        def gate_half(q, b, func):
            sums = sums_of(q, b)
            nc.vector.tensor_add(out=gates[:, q, half(b)], in0=sums[:], in1=gates[:, q, half(b)])
            nc.scalar.activation(out=gates[:, q, half(b)], in_=gates[:, q, half(b)], func=func)

        cell = keep.tile([P, H], F32)
        cell_tanh = keep.tile([P, H], F32)
        hidden = keep.tile([P, H], F32)
        forget, admit, fresh, expose = [gates[:, q, :] for q in (F_GATE, I_GATE, G_GATE, O_GATE)]

        def keep_part(b):
            nc.vector.tensor_mul(out=cell[:, half(b)], in0=forget[:, half(b)], in1=c_old[:, half(b)])

        def new_part(b):
            nc.vector.tensor_mul(out=fresh[:, half(b)], in0=admit[:, half(b)], in1=fresh[:, half(b)])

        def next_cell(b):
            nc.vector.tensor_add(out=cell[:, half(b)], in0=cell[:, half(b)], in1=fresh[:, half(b)])
            nc.scalar.activation(out=cell_tanh[:, half(b)], in_=cell[:, half(b)], func=ACT.Tanh)
            nc.sync.dma_start(out=out_1[:, half(b)], in_=cell[:, half(b)])

        gate_half(F_GATE, 0, ACT.Sigmoid)
        gate_half(F_GATE, 1, ACT.Sigmoid)
        gate_half(I_GATE, 0, ACT.Sigmoid)
        keep_part(0)
        gate_half(G_GATE, 0, ACT.Tanh)
        keep_part(1)
        gate_half(I_GATE, 1, ACT.Sigmoid)
        new_part(0)
        gate_half(G_GATE, 1, ACT.Tanh)
        next_cell(0)
        new_part(1)
        gate_half(O_GATE, 0, ACT.Sigmoid)
        next_cell(1)

        runs = []
        for r in range(BANK // RUN):
            sums = psum.tile([P, RUN], F32, name="sums", tag="bank")
            runs.append(sums)

        def last_pass(r, c):
            first = BANK + RUN * r
            nc.tensor.matmul_mx(
                out=runs[r][:],
                lhsT=x_codes[:, c, :].bitcast(FP8X4),
                lhsT_scale=x_planes[:, c, :],
                rhs=w_words[:, O_GATE, 1, c, 2 * RUN * r : 2 * RUN * (r + 1)].bitcast(FP4X4),
                rhs_scale=late_planes[:, c, first : first + RUN],
                start=(c == 0),
                stop=(c == PASSES - 1),
            )

        for r in range(BANK // RUN):
            for c in range(GROUPS):
                last_pass(r, c)
        for r in range(BANK // RUN):
            for c in range(GROUPS, PASSES):
                last_pass(r, c)
        pieces = [slice(BANK + QUARTER * k, BANK + QUARTER * (k + 1)) for k in range(BANK // QUARTER)]
        for k, cols in enumerate(pieces):
            for j in range(QUARTER // RUN):
                first = cols.start + RUN * j
                nc.vector.tensor_add(
                    out=expose[:, first : first + RUN],
                    in0=runs[k * (QUARTER // RUN) + j][:],
                    in1=expose[:, first : first + RUN],
                )
            nc.scalar.activation(out=expose[:, cols], in_=expose[:, cols], func=ACT.Sigmoid)
        for cols in [half(0)] + pieces:
            nc.vector.tensor_mul(out=hidden[:, cols], in0=expose[:, cols], in1=cell_tanh[:, cols])
            nc.sync.dma_start(out=out_0[:, cols], in_=hidden[:, cols])
